import numpy as np
import ml_dtypes


def mxq(x, axis, fmt="e4m3"):
    dtype, down = {"e4m3": (ml_dtypes.float8_e4m3fn, 7), "e5m2": (ml_dtypes.float8_e5m2, 14)}[fmt]
    v = np.moveaxis(np.asarray(x, np.float32).astype(ml_dtypes.bfloat16).astype(np.float64), axis, -1)
    blocks = v.reshape(v.shape[:-1] + (-1, 32))
    amax = np.abs(blocks).max(-1, keepdims=True)
    byte = np.maximum(np.where(amax > 0, np.frexp(amax)[1] - 1 + 127, 0) - down, 1)
    scale = np.exp2(byte - 127.0)
    codes = (blocks / scale).astype(np.float32).astype(dtype).astype(np.float64)
    return np.moveaxis((codes * scale).reshape(v.shape), -1, axis)


WIDE = False


def mx_kscale(k):
    if not WIDE:
        return np.ones(k)
    levels = np.array([20, -20, 10, -10, 0])
    a = np.random.permutation(np.resize(levels, k // 512 * 4)).reshape(k // 512, 4)
    idx = np.arange(k)
    return np.exp2(a[idx // 512, idx % 128 // 32])


BF16 = ml_dtypes.bfloat16


def bf(x):
    return np.asarray(x, np.float32).astype(BF16)


def f64(x):
    return np.asarray(x).astype(np.float64)


B, S, DIM, H, HD = 4, 2048, 512, 16, 64
E = H * HD
T = B * S


def rope_tables():
    inv_freq = 1.0 / (10000.0 ** (np.arange(0, HD, 2) / HD))
    freqs = np.outer(np.arange(S), inv_freq)
    emb = np.concatenate([freqs, freqs], axis=-1)
    return np.cos(emb)[None, None], np.sin(emb)[None, None]


def rotate_half(x):
    x1, x2 = np.split(x, 2, axis=-1)
    return np.concatenate([-x2, x1], axis=-1)


def rotate_half_t(y):
    y1, y2 = np.split(y, 2, axis=-1)
    return np.concatenate([y2, -y1], axis=-1)


def setup_inputs():
    s = mx_kscale(T).reshape(B, S)
    cos, sin = rope_tables()
    query = np.random.standard_normal((B, S, DIM)) * s[:, :, None]
    wq = np.random.standard_normal((E, DIM)) / np.sqrt(DIM)
    bq = np.random.standard_normal(E) * 0.1
    g = np.random.standard_normal((B, H, S, HD)) * np.exp2(np.random.randint(-12, 1, (B, 1, S, 1))) / s[:, None, :, None]
    return {"query": bf(query), "wq": bf(wq), "bq": bf(bq),
            "cos": bf(cos), "sin": bf(sin), "grad_out": bf(g)}


def reference(query, wq, bq, cos, sin, grad_out):
    g = f64(grad_out)
    dq = g * f64(cos) + rotate_half_t(g * f64(sin))
    dp = dq.transpose(0, 2, 1, 3).reshape(T, E)
    x = f64(query).reshape(T, DIM)
    return mxq(dp, 0, "e5m2").T @ mxq(x, 0, "e4m3")

@@ -1,0 +1,179 @@
+from contextlib import ExitStack
+
+import concourse.mybir as mybir
+from concourse.masks import make_identity
+
+BF16 = mybir.dt.bfloat16
+F32 = mybir.dt.float32
+U32 = mybir.dt.uint32
+U8 = mybir.dt.uint8
+E4M3_X4 = mybir.dt.float8_e4m3fn_x4
+E5M2_X4 = mybir.dt.float8_e5m2_x4
+MULT = mybir.AluOpType.mult
+ADD = mybir.AluOpType.add
+
+B, S, DIM, H, HD = 4, 2048, 512, 16, 64
+E = H * HD
+T = B * S
+HALF = HD // 2
+
+P = 128
+PACK = 4
+K_PASS = P * PACK
+GROUPS = S // K_PASS
+PASSES = B * GROUPS
+
+ROUNDS = 2
+HEADS = H // ROUNDS
+COLS = HEADS * HD
+M_TILES = COLS // P
+BANK_F32 = 512
+
+FLOPS = 2 * T * E * DIM
+BYTES = 2 * (T * DIM + T * E + 2 * S * HD) + 4 * E * DIM
+
+
+def load_table(nc, pool, table):
+    raw = pool.tile([P, GROUPS, PACK, HD], BF16, name="raw_table", tag="raw_table", bufs=2)
+    nc.sync.dma_start(
+        out=raw[:].rearrange("p j t d -> p j (t d)"),
+        in_=table[0, 0].rearrange("(j p t) d -> p j (t d)", p=P, t=PACK),
+    )
+    return raw
+
+
+def table_to_psum(nc, psum, identity, ordered, name):
+    bank = psum.tile([P, GROUPS, HD, PACK], BF16, name=name)
+    flat_in = ordered[:].rearrange("p j d t -> p (j d t)")
+    flat_out = bank[:].rearrange("p j d t -> p (j d t)")
+    for c in range(0, GROUPS * HD * PACK, BANK_F32):
+        nc.tensor.matmul(
+            out=flat_out[:, c : c + BANK_F32],
+            lhsT=identity[:],
+            rhs=flat_in[:, c : c + BANK_F32],
+            start=True,
+            stop=True,
+        )
+    return bank
+
+
+def tile_attention_pa_k_kernel(tc, query, wq, bq, cos, sin, grad_out, out):
+    nc = tc.nc
+    x_view = query.rearrange("b (j p t) i -> b j p (t i)", p=P, t=PACK)
+    g_view = grad_out.rearrange("b h (j p t) d -> b j p h (t d)", p=P, t=PACK)
+
+    with ExitStack() as stack:
+        keep = stack.enter_context(tc.tile_pool(name="keep", bufs=1))
+        g_pool = stack.enter_context(tc.tile_pool(name="g", bufs=4))
+        x_pool = stack.enter_context(tc.tile_pool(name="x", bufs=3))
+        prod_pool = stack.enter_context(tc.tile_pool(name="products", bufs=2))
+        dq_pool = stack.enter_context(tc.tile_pool(name="dq", bufs=1))
+        code_pool = stack.enter_context(tc.tile_pool(name="dp_codes", bufs=4))
+        res_pool = stack.enter_context(tc.tile_pool(name="result", bufs=4))
+        table_psum = stack.enter_context(tc.psum_pool(name="tables", bufs=1))
+        acc_psum = stack.enter_context(tc.psum_pool(name="acc", bufs=6))
+
+        cos_raw = load_table(nc, keep, cos)
+        sin_raw = load_table(nc, keep, sin)
+        identity = keep.tile([P, P], BF16)
+        make_identity(nc, identity[:])
+
+        cos_ordered = keep.tile([P, GROUPS, HD, PACK], BF16)
+        nc.vector.tensor_copy(out=cos_ordered[:], in_=cos_raw[:].rearrange("p j t d -> p j d t"))
+        sin_view = sin_raw[:].rearrange("p j t d -> p j d t")
+        sin_signed = keep.tile([P, GROUPS, HD, PACK], BF16)
+        nc.vector.tensor_scalar_mul(sin_signed[:, :, :HALF, :], sin_view[:, :, :HALF, :], -1.0)
+        nc.vector.tensor_copy(out=sin_signed[:, :, HALF:, :], in_=sin_view[:, :, HALF:, :])
+
+        cos_bank = table_to_psum(nc, table_psum, identity, cos_ordered, "cos_bank")
+        sin_bank = table_to_psum(nc, table_psum, identity, sin_signed, "sin_bank")
+
+        x_codes = keep.tile([P, PASSES, DIM], U32, align_bytes=64)
+        x_scales = keep.tile([P, PASSES, DIM], U8, align_bytes=64)
+
+        units = [(r, c) for r in range(ROUNDS) for c in range(PASSES)]
+
+        def quantise_x(c):
+            x_raw = x_pool.tile([P, PACK, DIM], BF16)
+            nc.sync.dma_start(out=x_raw[:].rearrange("p t i -> p (t i)"), in_=x_view[c // GROUPS, c % GROUPS])
+            x_grouped = x_pool.tile([P, DIM, PACK], BF16, align_bytes=64)
+            nc.scalar.copy(out=x_grouped[:], in_=x_raw[:].rearrange("p t i -> p i t"))
+            nc.vector.quantize_mx(
+                out=x_codes[:, c, :].bitcast(E4M3_X4),
+                scales=x_scales[:, c, :],
+                in_=x_grouped[:].rearrange("p i t -> p (i t)"),
+            )
+
+        def products(r, c):
+            b, j = c // GROUPS, c % GROUPS
+            g_raw = g_pool.tile([P, HEADS, PACK, HD], BF16)
+            nc.sync.dma_start(
+                out=g_raw[:].rearrange("p h t d -> p h (t d)"),
+                in_=g_view[b, j][:, r * HEADS : (r + 1) * HEADS, :],
+            )
+            g = g_raw[:].rearrange("p h t d -> p h d t")
+            with_cos = prod_pool.tile([P, HEADS, HD, PACK], F32)
+            nc.vector.tensor_tensor(
+                out=with_cos[:],
+                in0=g,
+                in1=cos_bank[:, j].unsqueeze(1).to_broadcast([P, HEADS, HD, PACK]),
+                op=MULT,
+            )
+            with_sin = prod_pool.tile([P, HEADS, HD, PACK], F32)
+            for src, dst in ((slice(0, HALF), slice(HALF, HD)), (slice(HALF, HD), slice(0, HALF))):
+                nc.vector.tensor_tensor(
+                    out=with_sin[:, :, dst, :],
+                    in0=g[:, :, src, :],
+                    in1=sin_bank[:, j, src, :].unsqueeze(1).to_broadcast([P, HEADS, HALF, PACK]),
+                    op=MULT,
+                )
+            return with_cos, with_sin
+
+        def add(with_cos, with_sin):
+            dq = dq_pool.tile([P, HEADS, HD, PACK], BF16, align_bytes=64)
+            nc.gpsimd.tensor_tensor(out=dq[:], in0=with_cos[:], in1=with_sin[:], op=ADD)
+            return dq
+
+        def quantise_and_multiply(c, dq, acc):
+            dp_codes = code_pool.tile([P, COLS], U32, align_bytes=64)
+            dp_scales = code_pool.tile([P, COLS], U8, align_bytes=64)
+            nc.vector.quantize_mx(
+                out=dp_codes[:].bitcast(E5M2_X4),
+                scales=dp_scales[:],
+                in_=dq[:].rearrange("p h d t -> p (h d t)"),
+            )
+            for m in range(M_TILES):
+                cols = slice(m * P, (m + 1) * P)
+                nc.tensor.matmul_mx(
+                    out=acc[m][:],
+                    lhsT=dp_codes[:, cols].bitcast(E5M2_X4),
+                    lhsT_scale=dp_scales[:, cols],
+                    rhs=x_codes[:, c, :].bitcast(E4M3_X4),
+                    rhs_scale=x_scales[:, c, :],
+                    start=(c == 0),
+                    stop=(c == PASSES - 1),
+                )
+
+        def store_round(r, acc):
+            for m in range(M_TILES):
+                rows = slice(r * COLS + m * P, r * COLS + (m + 1) * P)
+                result = res_pool.tile([P, DIM], F32)
+                nc.scalar.copy(out=result[:], in_=acc[m][:])
+                nc.scalar.dma_start(out=out[rows, :], in_=result[:])
+
+        with tc.manual_schedule():
+            acc = None
+            added = None
+            for r, c in units:
+                factors = products(r, c)
+                if r == 0:
+                    quantise_x(c)
+                if added is not None:
+                    quantise_and_multiply(added[1], added[2], acc)
+                    if added[1] == PASSES - 1:
+                        store_round(added[0], acc)
+                if c == 0:
+                    acc = [acc_psum.tile([P, DIM], F32, name="acc%d" % m, tag="acc") for m in range(M_TILES)]
+                added = (r, c, add(*factors))
+            quantise_and_multiply(added[1], added[2], acc)
+            store_round(added[0], acc)

@@ -29,6 +29,10 @@ COLS = HEADS * HD
 M_TILES = COLS // P
 BANK_F32 = 512
 
+PAIR = 2
+UNITS = PASSES // PAIR
+GPSIMD_HEADS = HEADS - 1
+
 FLOPS = 2 * T * E * DIM
 BYTES = 2 * (T * DIM + T * E + 2 * S * HD) + 4 * E * DIM
 
@@ -59,24 +63,27 @@ def table_to_psum(nc, psum, identity, ordered, name):
 
 def tile_attention_pa_k_kernel(tc, query, wq, bq, cos, sin, grad_out, out):
     nc = tc.nc
-    x_view = query.rearrange("b (j p t) i -> b j p (t i)", p=P, t=PACK)
+    x_view = query.rearrange("b (j p t) i -> (b j) p (t i)", p=P, t=PACK)
     g_view = grad_out.rearrange("b h (j p t) d -> b j p h (t d)", p=P, t=PACK)
 
     with ExitStack() as stack:
         keep = stack.enter_context(tc.tile_pool(name="keep", bufs=1))
-        g_pool = stack.enter_context(tc.tile_pool(name="g", bufs=4))
-        x_pool = stack.enter_context(tc.tile_pool(name="x", bufs=3))
+        g_pool = stack.enter_context(tc.tile_pool(name="g", bufs=3))
+        x_pool = stack.enter_context(tc.tile_pool(name="x", bufs=2))
         prod_pool = stack.enter_context(tc.tile_pool(name="products", bufs=2))
         dq_pool = stack.enter_context(tc.tile_pool(name="dq", bufs=1))
-        code_pool = stack.enter_context(tc.tile_pool(name="dp_codes", bufs=4))
+        code_pool = stack.enter_context(tc.tile_pool(name="dp_codes", bufs=3))
         res_pool = stack.enter_context(tc.tile_pool(name="result", bufs=4))
         table_psum = stack.enter_context(tc.psum_pool(name="tables", bufs=1))
-        acc_psum = stack.enter_context(tc.psum_pool(name="acc", bufs=6))
+        sum_psum = stack.enter_context(tc.psum_pool(name="sums", bufs=2))
+        acc_psum = stack.enter_context(tc.psum_pool(name="acc", bufs=M_TILES))
 
         cos_raw = load_table(nc, keep, cos)
         sin_raw = load_table(nc, keep, sin)
         identity = keep.tile([P, P], BF16)
         make_identity(nc, identity[:])
+        identity_f32 = keep.tile([P, P], F32)
+        make_identity(nc, identity_f32[:])
 
         cos_ordered = keep.tile([P, GROUPS, HD, PACK], BF16)
         nc.vector.tensor_copy(out=cos_ordered[:], in_=cos_raw[:].rearrange("p j t d -> p j d t"))
@@ -91,68 +98,91 @@ def tile_attention_pa_k_kernel(tc, query, wq, bq, cos, sin, grad_out, out):
         x_codes = keep.tile([P, PASSES, DIM], U32, align_bytes=64)
         x_scales = keep.tile([P, PASSES, DIM], U8, align_bytes=64)
 
-        units = [(r, c) for r in range(ROUNDS) for c in range(PASSES)]
 
-        def quantise_x(c):
-            x_raw = x_pool.tile([P, PACK, DIM], BF16)
-            nc.sync.dma_start(out=x_raw[:].rearrange("p t i -> p (t i)"), in_=x_view[c // GROUPS, c % GROUPS])
-            x_grouped = x_pool.tile([P, DIM, PACK], BF16, align_bytes=64)
-            nc.scalar.copy(out=x_grouped[:], in_=x_raw[:].rearrange("p t i -> p i t"))
-            nc.vector.quantize_mx(
-                out=x_codes[:, c, :].bitcast(E4M3_X4),
-                scales=x_scales[:, c, :],
-                in_=x_grouped[:].rearrange("p i t -> p (i t)"),
-            )
-
-        def products(r, c):
-            b, j = c // GROUPS, c % GROUPS
-            g_raw = g_pool.tile([P, HEADS, PACK, HD], BF16)
-            nc.sync.dma_start(
-                out=g_raw[:].rearrange("p h t d -> p h (t d)"),
-                in_=g_view[b, j][:, r * HEADS : (r + 1) * HEADS, :],
-            )
-            g = g_raw[:].rearrange("p h t d -> p h d t")
-            with_cos = prod_pool.tile([P, HEADS, HD, PACK], F32)
-            nc.vector.tensor_tensor(
-                out=with_cos[:],
-                in0=g,
-                in1=cos_bank[:, j].unsqueeze(1).to_broadcast([P, HEADS, HD, PACK]),
-                op=MULT,
-            )
-            with_sin = prod_pool.tile([P, HEADS, HD, PACK], F32)
-            for src, dst in ((slice(0, HALF), slice(HALF, HD)), (slice(HALF, HD), slice(0, HALF))):
+        def products(r, u):
+            g_raw = g_pool.tile([P, PAIR, HEADS, PACK, HD], BF16)
+            with_cos = prod_pool.tile([P, PAIR, HEADS, HD, PACK], F32)
+            with_sin = prod_pool.tile([P, PAIR, HEADS, HD, PACK], F32)
+            for k in range(PAIR):
+                b, j = (PAIR * u + k) // GROUPS, (PAIR * u + k) % GROUPS
+                nc.sync.dma_start(
+                    out=g_raw[:, k].rearrange("p h t d -> p h (t d)"),
+                    in_=g_view[b, j][:, r * HEADS : (r + 1) * HEADS, :],
+                )
+                g = g_raw[:, k].rearrange("p h t d -> p h d t")
                 nc.vector.tensor_tensor(
-                    out=with_sin[:, :, dst, :],
-                    in0=g[:, :, src, :],
-                    in1=sin_bank[:, j, src, :].unsqueeze(1).to_broadcast([P, HEADS, HALF, PACK]),
+                    out=with_cos[:, k],
+                    in0=g,
+                    in1=cos_bank[:, j].unsqueeze(1).to_broadcast([P, HEADS, HD, PACK]),
                     op=MULT,
                 )
+                for src, dst in ((slice(0, HALF), slice(HALF, HD)), (slice(HALF, HD), slice(0, HALF))):
+                    nc.vector.tensor_tensor(
+                        out=with_sin[:, k, :, dst, :],
+                        in0=g[:, :, src, :],
+                        in1=sin_bank[:, j, src, :].unsqueeze(1).to_broadcast([P, HEADS, HALF, PACK]),
+                        op=MULT,
+                    )
             return with_cos, with_sin
 
         def add(with_cos, with_sin):
-            dq = dq_pool.tile([P, HEADS, HD, PACK], BF16, align_bytes=64)
-            nc.gpsimd.tensor_tensor(out=dq[:], in0=with_cos[:], in1=with_sin[:], op=ADD)
+            dq = dq_pool.tile([P, PAIR, HEADS, HD, PACK], BF16, align_bytes=64)
+            nc.gpsimd.tensor_tensor(
+                out=dq[:, :, :GPSIMD_HEADS],
+                in0=with_cos[:, :, :GPSIMD_HEADS],
+                in1=with_sin[:, :, :GPSIMD_HEADS],
+                op=ADD,
+            )
+            last_head = sum_psum.tile([P, PAIR, HD, PACK], F32)
+            for k in range(PAIR):
+                for term, first in ((with_cos, True), (with_sin, False)):
+                    nc.tensor.matmul(
+                        out=last_head[:, k].rearrange("p d t -> p (d t)"),
+                        lhsT=identity_f32[:],
+                        rhs=term[:, k, GPSIMD_HEADS].rearrange("p d t -> p (d t)"),
+                        start=first,
+                        stop=not first,
+                    )
+            nc.scalar.copy(out=dq[:, :, GPSIMD_HEADS], in_=last_head[:])
             return dq
 
-        def quantise_and_multiply(c, dq, acc):
-            dp_codes = code_pool.tile([P, COLS], U32, align_bytes=64)
-            dp_scales = code_pool.tile([P, COLS], U8, align_bytes=64)
+        def regroup_x(u):
+            x_raw = x_pool.tile([P, PAIR, PACK, DIM], BF16)
+            x_grouped = x_pool.tile([P, PAIR, DIM, PACK], BF16, align_bytes=64)
+            for k in range(PAIR):
+                nc.sync.dma_start(out=x_raw[:, k].rearrange("p t i -> p (t i)"), in_=x_view[PAIR * u + k])
+                nc.scalar.copy(out=x_grouped[:, k], in_=x_raw[:, k].rearrange("p t i -> p i t"))
+            return x_grouped
+
+        def quantise_x(u, x_grouped):
+            both = slice(PAIR * u, PAIR * (u + 1))
             nc.vector.quantize_mx(
-                out=dp_codes[:].bitcast(E5M2_X4),
-                scales=dp_scales[:],
-                in_=dq[:].rearrange("p h d t -> p (h d t)"),
+                out=x_codes[:, both, :].rearrange("p c i -> p (c i)").bitcast(E4M3_X4),
+                scales=x_scales[:, both, :].rearrange("p c i -> p (c i)"),
+                in_=x_grouped[:].rearrange("p c i t -> p (c i t)"),
             )
-            for m in range(M_TILES):
-                cols = slice(m * P, (m + 1) * P)
-                nc.tensor.matmul_mx(
-                    out=acc[m][:],
-                    lhsT=dp_codes[:, cols].bitcast(E5M2_X4),
-                    lhsT_scale=dp_scales[:, cols],
-                    rhs=x_codes[:, c, :].bitcast(E4M3_X4),
-                    rhs_scale=x_scales[:, c, :],
-                    start=(c == 0),
-                    stop=(c == PASSES - 1),
-                )
+
+        def quantise_and_multiply(u, dq, acc):
+            dp_codes = code_pool.tile([P, PAIR, COLS], U32, align_bytes=64)
+            dp_scales = code_pool.tile([P, PAIR, COLS], U8, align_bytes=64)
+            nc.vector.quantize_mx(
+                out=dp_codes[:].rearrange("p c w -> p (c w)").bitcast(E5M2_X4),
+                scales=dp_scales[:].rearrange("p c w -> p (c w)"),
+                in_=dq[:].rearrange("p c h d t -> p (c h d t)"),
+            )
+            for k in range(PAIR):
+                c = PAIR * u + k
+                for m in range(M_TILES):
+                    cols = slice(m * P, (m + 1) * P)
+                    nc.tensor.matmul_mx(
+                        out=acc[m][:],
+                        lhsT=dp_codes[:, k, cols].bitcast(E5M2_X4),
+                        lhsT_scale=dp_scales[:, k, cols],
+                        rhs=x_codes[:, c, :].bitcast(E4M3_X4),
+                        rhs_scale=x_scales[:, c, :],
+                        start=(c == 0),
+                        stop=(c == PASSES - 1),
+                    )
 
         def store_round(r, acc):
             for m in range(M_TILES):
@@ -161,19 +191,23 @@ def tile_attention_pa_k_kernel(tc, query, wq, bq, cos, sin, grad_out, out):
                 nc.scalar.copy(out=result[:], in_=acc[m][:])
                 nc.scalar.dma_start(out=out[rows, :], in_=result[:])
 
+        def finish(r, u, dq, x_grouped, acc):
+            if r == 0:
+                quantise_x(u, x_grouped)
+            quantise_and_multiply(u, dq, acc)
+            if u == UNITS - 1:
+                store_round(r, acc)
+
         with tc.manual_schedule():
             acc = None
             added = None
-            for r, c in units:
-                factors = products(r, c)
-                if r == 0:
-                    quantise_x(c)
-                if added is not None:
-                    quantise_and_multiply(added[1], added[2], acc)
-                    if added[1] == PASSES - 1:
-                        store_round(added[0], acc)
-                if c == 0:
-                    acc = [acc_psum.tile([P, DIM], F32, name="acc%d" % m, tag="acc") for m in range(M_TILES)]
-                added = (r, c, add(*factors))
-            quantise_and_multiply(added[1], added[2], acc)
-            store_round(added[0], acc)
+            for r in range(ROUNDS):
+                for u in range(UNITS):
+                    factors = products(r, u)
+                    if added is not None:
+                        finish(*added, acc)
+                    if u == 0:
+                        acc = [acc_psum.tile([P, DIM], F32, name="acc%d" % m, tag="acc") for m in range(M_TILES)]
+                    x_grouped = regroup_x(u) if r == 0 else None
+                    added = (r, u, add(*factors), x_grouped)
+            finish(*added, acc)

@@ -68,6 +68,7 @@ def tile_attention_pa_k_kernel(tc, query, wq, bq, cos, sin, grad_out, out):
 
     with ExitStack() as stack:
         keep = stack.enter_context(tc.tile_pool(name="keep", bufs=1))
+        raw_pool = stack.enter_context(tc.tile_pool(name="g_raw", bufs=2))
         g_pool = stack.enter_context(tc.tile_pool(name="g", bufs=3))
         x_pool = stack.enter_context(tc.tile_pool(name="x", bufs=2))
         prod_pool = stack.enter_context(tc.tile_pool(name="products", bufs=2))
@@ -99,30 +100,38 @@ def tile_attention_pa_k_kernel(tc, query, wq, bq, cos, sin, grad_out, out):
         x_scales = keep.tile([P, PASSES, DIM], U8, align_bytes=64)
 
 
-        def products(r, u):
-            g_raw = g_pool.tile([P, PAIR, HEADS, PACK, HD], BF16)
-            with_cos = prod_pool.tile([P, PAIR, HEADS, HD, PACK], F32)
-            with_sin = prod_pool.tile([P, PAIR, HEADS, HD, PACK], F32)
+        def reorder_g(r, u):
+            g_raw = raw_pool.tile([P, PAIR, HEADS, PACK, HD], BF16)
             for k in range(PAIR):
                 b, j = (PAIR * u + k) // GROUPS, (PAIR * u + k) % GROUPS
                 nc.sync.dma_start(
                     out=g_raw[:, k].rearrange("p h t d -> p h (t d)"),
                     in_=g_view[b, j][:, r * HEADS : (r + 1) * HEADS, :],
                 )
-                g = g_raw[:, k].rearrange("p h t d -> p h d t")
+            g = g_pool.tile([P, PAIR, HEADS, HD, PACK], BF16)
+            nc.scalar.copy(
+                out=g[:].rearrange("p k h d t -> p (k h) d t"),
+                in_=g_raw[:].rearrange("p k h t d -> p (k h) d t"),
+            )
+            return g
+
+        def products(u, g):
+            groups = slice((PAIR * u) % GROUPS, (PAIR * u) % GROUPS + PAIR)
+            with_cos = prod_pool.tile([P, PAIR, HEADS, HD, PACK], F32)
+            nc.vector.tensor_tensor(
+                out=with_cos[:],
+                in0=g[:],
+                in1=cos_bank[:, groups].unsqueeze(2).to_broadcast([P, PAIR, HEADS, HD, PACK]),
+                op=MULT,
+            )
+            with_sin = prod_pool.tile([P, PAIR, HEADS, HD, PACK], F32)
+            for src, dst in ((slice(0, HALF), slice(HALF, HD)), (slice(HALF, HD), slice(0, HALF))):
                 nc.vector.tensor_tensor(
-                    out=with_cos[:, k],
-                    in0=g,
-                    in1=cos_bank[:, j].unsqueeze(1).to_broadcast([P, HEADS, HD, PACK]),
+                    out=with_sin[:, :, :, dst, :],
+                    in0=g[:, :, :, src, :],
+                    in1=sin_bank[:, groups, src, :].unsqueeze(2).to_broadcast([P, PAIR, HEADS, HALF, PACK]),
                     op=MULT,
                 )
-                for src, dst in ((slice(0, HALF), slice(HALF, HD)), (slice(HALF, HD), slice(0, HALF))):
-                    nc.vector.tensor_tensor(
-                        out=with_sin[:, k, :, dst, :],
-                        in0=g[:, :, src, :],
-                        in1=sin_bank[:, j, src, :].unsqueeze(1).to_broadcast([P, HEADS, HALF, PACK]),
-                        op=MULT,
-                    )
             return with_cos, with_sin
 
         def add(with_cos, with_sin):
@@ -198,16 +207,21 @@ def tile_attention_pa_k_kernel(tc, query, wq, bq, cos, sin, grad_out, out):
             if u == UNITS - 1:
                 store_round(r, acc)
 
+        units = [(r, u) for r in range(ROUNDS) for u in range(UNITS)]
+        AHEAD = 2
         with tc.manual_schedule():
+            reordered = [reorder_g(*unit) for unit in units[:AHEAD]]
+            x_grouped = regroup_x(0)
             acc = None
             added = None
-            for r in range(ROUNDS):
-                for u in range(UNITS):
-                    factors = products(r, u)
-                    if added is not None:
-                        finish(*added, acc)
-                    if u == 0:
-                        acc = [acc_psum.tile([P, DIM], F32, name="acc%d" % m, tag="acc") for m in range(M_TILES)]
-                    x_grouped = regroup_x(u) if r == 0 else None
-                    added = (r, u, add(*factors), x_grouped)
+            for n, (r, u) in enumerate(units):
+                factors = products(u, reordered[n])
+                if added is not None:
+                    finish(*added, acc)
+                if u == 0:
+                    acc = [acc_psum.tile([P, DIM], F32, name="acc%d" % m, tag="acc") for m in range(M_TILES)]
+                if n + AHEAD < len(units):
+                    reordered.append(reorder_g(*units[n + AHEAD]))
+                added = (r, u, add(*factors), x_grouped)
+                x_grouped = regroup_x(u + 1) if r == 0 and u + 1 < UNITS else None
             finish(*added, acc)

@@ -10,7 +10,6 @@ U8 = mybir.dt.uint8
 E4M3_X4 = mybir.dt.float8_e4m3fn_x4
 E5M2_X4 = mybir.dt.float8_e5m2_x4
 MULT = mybir.AluOpType.mult
-ADD = mybir.AluOpType.add
 
 B, S, DIM, H, HD = 4, 2048, 512, 16, 64
 E = H * HD
@@ -22,206 +21,255 @@ PACK = 4
 K_PASS = P * PACK
 GROUPS = S // K_PASS
 PASSES = B * GROUPS
+PAIRS = HD // 2
 
 ROUNDS = 2
 HEADS = H // ROUNDS
 COLS = HEADS * HD
 M_TILES = COLS // P
-BANK_F32 = 512
-
-PAIR = 2
-UNITS = PASSES // PAIR
-GPSIMD_HEADS = HEADS - 1
+QUAD = 4
+UNITS = ROUNDS * PASSES * (HEADS // QUAD)
+STEPS = ROUNDS * PASSES
+X_PIECES = 4
 
 FLOPS = 2 * T * E * DIM
 BYTES = 2 * (T * DIM + T * E + 2 * S * HD) + 4 * E * DIM
 
 
-def load_table(nc, pool, table):
-    raw = pool.tile([P, GROUPS, PACK, HD], BF16, name="raw_table", tag="raw_table", bufs=2)
-    nc.sync.dma_start(
-        out=raw[:].rearrange("p j t d -> p j (t d)"),
-        in_=table[0, 0].rearrange("(j p t) d -> p j (t d)", p=P, t=PACK),
-    )
-    return raw
+def on_gpsimd(n):
+    return n % 3 == 2
 
 
-def table_to_psum(nc, psum, identity, ordered, name):
-    bank = psum.tile([P, GROUPS, HD, PACK], BF16, name=name)
-    flat_in = ordered[:].rearrange("p j d t -> p (j d t)")
-    flat_out = bank[:].rearrange("p j d t -> p (j d t)")
-    for c in range(0, GROUPS * HD * PACK, BANK_F32):
-        nc.tensor.matmul(
-            out=flat_out[:, c : c + BANK_F32],
-            lhsT=identity[:],
-            rhs=flat_in[:, c : c + BANK_F32],
-            start=True,
-            stop=True,
-        )
-    return bank
+def unit_added_at(i):
+    n = i if i % 3 != 2 else i - 3
+    return n if 0 <= n < UNITS else None
 
 
 def tile_attention_pa_k_kernel(tc, query, wq, bq, cos, sin, grad_out, out):
     nc = tc.nc
     x_view = query.rearrange("b (j p t) i -> (b j) p (t i)", p=P, t=PACK)
     g_view = grad_out.rearrange("b h (j p t) d -> b j p h (t d)", p=P, t=PACK)
+    out_view = out.rearrange("(a q e) i -> a e q i", q=PAIRS, e=2)
 
     with ExitStack() as stack:
         keep = stack.enter_context(tc.tile_pool(name="keep", bufs=1))
-        raw_pool = stack.enter_context(tc.tile_pool(name="g_raw", bufs=2))
-        g_pool = stack.enter_context(tc.tile_pool(name="g", bufs=3))
-        x_pool = stack.enter_context(tc.tile_pool(name="x", bufs=2))
-        prod_pool = stack.enter_context(tc.tile_pool(name="products", bufs=2))
-        dq_pool = stack.enter_context(tc.tile_pool(name="dq", bufs=1))
-        code_pool = stack.enter_context(tc.tile_pool(name="dp_codes", bufs=3))
+        raw_pool = stack.enter_context(tc.tile_pool(name="g_raw", bufs=4))
+        copy_pool = stack.enter_context(tc.tile_pool(name="g_copy", bufs=2))
+        prod_pool = stack.enter_context(tc.tile_pool(name="products", bufs=6))
+        x_pool = stack.enter_context(tc.tile_pool(name="x", bufs=3))
+        dq_pool = stack.enter_context(tc.tile_pool(name="dq", bufs=4))
+        code_pool = stack.enter_context(tc.tile_pool(name="dp_codes", bufs=4))
         res_pool = stack.enter_context(tc.tile_pool(name="result", bufs=4))
-        table_psum = stack.enter_context(tc.psum_pool(name="tables", bufs=1))
-        sum_psum = stack.enter_context(tc.psum_pool(name="sums", bufs=2))
+        turn_psum = stack.enter_context(tc.psum_pool(name="turned", bufs=2))
+        total_psum = stack.enter_context(tc.psum_pool(name="totals", bufs=2))
         acc_psum = stack.enter_context(tc.psum_pool(name="acc", bufs=M_TILES))
 
-        cos_raw = load_table(nc, keep, cos)
-        sin_raw = load_table(nc, keep, sin)
-        identity = keep.tile([P, P], BF16)
+        def load_table(table):
+            raw = keep.tile([P, GROUPS, PACK, HD], BF16, name="raw_table", tag="raw_table", bufs=2)
+            nc.sync.dma_start(
+                out=raw[:].rearrange("p j t d -> p j (t d)"),
+                in_=table[0, 0].rearrange("(j p t) d -> p j (t d)", p=P, t=PACK),
+            )
+            return raw
+
+        cos_raw = load_table(cos)
+        sin_raw = load_table(sin)
+
+        identity = keep.tile([P, P], F32)
         make_identity(nc, identity[:])
-        identity_f32 = keep.tile([P, P], F32)
-        make_identity(nc, identity_f32[:])
+        swap = keep.tile([P, P], F32)
+        identity_blocks = identity[:].rearrange("k (t u w) -> k t u w", t=PACK, u=2)
+        swap_blocks = swap[:].rearrange("k (t u w) -> k t u w", t=PACK, u=2)
+        nc.vector.tensor_copy(out=swap_blocks[:, :, 0, :], in_=identity_blocks[:, :, 1, :])
+        nc.vector.tensor_copy(out=swap_blocks[:, :, 1, :], in_=identity_blocks[:, :, 0, :])
 
-        cos_ordered = keep.tile([P, GROUPS, HD, PACK], BF16)
-        nc.vector.tensor_copy(out=cos_ordered[:], in_=cos_raw[:].rearrange("p j t d -> p j d t"))
-        sin_view = sin_raw[:].rearrange("p j t d -> p j d t")
-        sin_signed = keep.tile([P, GROUPS, HD, PACK], BF16)
-        nc.vector.tensor_scalar_mul(sin_signed[:, :, :HALF, :], sin_view[:, :, :HALF, :], -1.0)
-        nc.vector.tensor_copy(out=sin_signed[:, :, HALF:, :], in_=sin_view[:, :, HALF:, :])
+        sin_signed = keep.tile([P, GROUPS, PACK, HD], BF16)
+        nc.vector.tensor_scalar_mul(sin_signed[:, :, :, :HALF], sin_raw[:, :, :, :HALF], -1.0)
+        nc.vector.tensor_copy(out=sin_signed[:, :, :, HALF:], in_=sin_raw[:, :, :, HALF:])
 
-        cos_bank = table_to_psum(nc, table_psum, identity, cos_ordered, "cos_bank")
-        sin_bank = table_to_psum(nc, table_psum, identity, sin_signed, "sin_bank")
+        def parities_apart(words, count):
+            flat = words.rearrange("k c p -> k (c p)").bitcast(BF16)
+            return flat.rearrange("k (c p e) -> k c e p", c=count, e=2)
+
+        def turn_table(raw, name):
+            bank = turn_psum.tile([P, GROUPS, P], F32, name="g_t", tag="g_t")
+            for j in range(GROUPS):
+                nc.tensor.transpose(bank[:, j, :], raw[:, j].rearrange("p t d -> p (t d)").bitcast(F32), identity[:])
+            table = keep.tile([P, GROUPS, 2, P], BF16, name=name)
+            nc.vector.tensor_copy(out=table[:], in_=parities_apart(bank[:], GROUPS))
+            return table
+
+        cos_t = turn_table(cos_raw, "cos_t")
+        sin_t = turn_table(sin_signed, "sin_t")
 
         x_codes = keep.tile([P, PASSES, DIM], U32, align_bytes=64)
         x_scales = keep.tile([P, PASSES, DIM], U8, align_bytes=64)
 
+        raws, products, dqs, codes, x_raws, x_groupeds = {}, {}, {}, {}, {}, {}
+        accs = []
 
-        def reorder_g(r, u):
-            g_raw = raw_pool.tile([P, PAIR, HEADS, PACK, HD], BF16)
-            for k in range(PAIR):
-                b, j = (PAIR * u + k) // GROUPS, (PAIR * u + k) % GROUPS
-                nc.sync.dma_start(
-                    out=g_raw[:, k].rearrange("p h t d -> p h (t d)"),
-                    in_=g_view[b, j][:, r * HEADS : (r + 1) * HEADS, :],
-                )
-            g = g_pool.tile([P, PAIR, HEADS, HD, PACK], BF16)
-            nc.scalar.copy(
-                out=g[:].rearrange("p k h d t -> p (k h) d t"),
-                in_=g_raw[:].rearrange("p k h t d -> p (k h) d t"),
-            )
-            return g
+        def load_g(s):
+            r, c = divmod(s, PASSES)
+            b, j = divmod(c, GROUPS)
+            g_raw = raw_pool.tile([P, HEADS, PACK * HD], BF16, name="g_raw")
+            nc.sync.dma_start(out=g_raw[:], in_=g_view[b, j][:, r * HEADS : (r + 1) * HEADS, :])
+            raws[s] = g_raw
 
-        def products(u, g):
-            groups = slice((PAIR * u) % GROUPS, (PAIR * u) % GROUPS + PAIR)
-            with_cos = prod_pool.tile([P, PAIR, HEADS, HD, PACK], F32)
-            nc.vector.tensor_tensor(
-                out=with_cos[:],
-                in0=g[:],
-                in1=cos_bank[:, groups].unsqueeze(2).to_broadcast([P, PAIR, HEADS, HD, PACK]),
-                op=MULT,
-            )
-            with_sin = prod_pool.tile([P, PAIR, HEADS, HD, PACK], F32)
-            for src, dst in ((slice(0, HALF), slice(HALF, HD)), (slice(HALF, HD), slice(0, HALF))):
-                nc.vector.tensor_tensor(
-                    out=with_sin[:, :, :, dst, :],
-                    in0=g[:, :, :, src, :],
-                    in1=sin_bank[:, groups, src, :].unsqueeze(2).to_broadcast([P, PAIR, HEADS, HALF, PACK]),
-                    op=MULT,
-                )
-            return with_cos, with_sin
-
-        def add(with_cos, with_sin):
-            dq = dq_pool.tile([P, PAIR, HEADS, HD, PACK], BF16, align_bytes=64)
-            nc.gpsimd.tensor_tensor(
-                out=dq[:, :, :GPSIMD_HEADS],
-                in0=with_cos[:, :, :GPSIMD_HEADS],
-                in1=with_sin[:, :, :GPSIMD_HEADS],
-                op=ADD,
-            )
-            last_head = sum_psum.tile([P, PAIR, HD, PACK], F32)
-            for k in range(PAIR):
-                for term, first in ((with_cos, True), (with_sin, False)):
-                    nc.tensor.matmul(
-                        out=last_head[:, k].rearrange("p d t -> p (d t)"),
-                        lhsT=identity_f32[:],
-                        rhs=term[:, k, GPSIMD_HEADS].rearrange("p d t -> p (d t)"),
-                        start=first,
-                        stop=not first,
+        def turn_and_multiply(n):
+            s, a = divmod(n, 2)
+            j = s % GROUPS
+            g_t = turn_psum.tile([P, QUAD, P], F32, name="g_t", tag="g_t")
+            for h in range(QUAD):
+                nc.tensor.transpose(g_t[:, h, :], raws[s][:, a * QUAD + h, :].bitcast(F32), identity[:])
+            with_cos = prod_pool.tile([P, QUAD, 2, P], F32, name="with_cos")
+            with_sin = prod_pool.tile([P, QUAD, 2, P], F32, name="with_sin")
+            terms = ((cos_t, with_cos), (sin_t, with_sin))
+            if on_gpsimd(n):
+                g_copy = copy_pool.tile([P, QUAD, P], F32, name="g_copy")
+                nc.scalar.copy(out=g_copy[:], in_=g_t[:])
+                values = parities_apart(g_copy[:], QUAD)
+                for h in range(0, QUAD, 2):
+                    for table, product in terms:
+                        nc.gpsimd.tensor_tensor(
+                            out=product[:, h : h + 2],
+                            in0=values[:, h : h + 2],
+                            in1=table[:, j].unsqueeze(1).to_broadcast([P, 2, 2, P]),
+                            op=MULT,
+                        )
+            else:
+                values = parities_apart(g_t[:], QUAD)
+                for table, product in terms:
+                    nc.vector.tensor_tensor(
+                        out=product[:],
+                        in0=values,
+                        in1=table[:, j].unsqueeze(1).to_broadcast([P, QUAD, 2, P]),
+                        op=MULT,
                     )
-            nc.scalar.copy(out=dq[:, :, GPSIMD_HEADS], in_=last_head[:])
-            return dq
+            products[n] = (with_cos, with_sin)
 
-        def regroup_x(u):
-            x_raw = x_pool.tile([P, PAIR, PACK, DIM], BF16)
-            x_grouped = x_pool.tile([P, PAIR, DIM, PACK], BF16, align_bytes=64)
-            for k in range(PAIR):
-                nc.sync.dma_start(out=x_raw[:, k].rearrange("p t i -> p (t i)"), in_=x_view[PAIR * u + k])
-                nc.scalar.copy(out=x_grouped[:, k], in_=x_raw[:, k].rearrange("p t i -> p i t"))
-            return x_grouped
+        def add_up(n):
+            s, a = divmod(n, 2)
+            if s not in dqs:
+                dqs[s] = dq_pool.tile([P, COLS, PACK], BF16, name="dq", align_bytes=64)
+            with_cos, with_sin = products[n]
+            for half in range(2):
+                total = total_psum.tile([P, 4, P], F32, name="total")
+                for h2 in range(2):
+                    for e in range(2):
+                        h = 2 * half + h2
+                        nc.tensor.matmul(
+                            out=total[:, 2 * h2 + e, :], lhsT=with_cos[:, h, e, :], rhs=identity[:],
+                            is_transpose=True, start=True, stop=False,
+                        )
+                        nc.tensor.matmul(
+                            out=total[:, 2 * h2 + e, :], lhsT=with_sin[:, h, e, :], rhs=swap[:],
+                            is_transpose=True, start=False, stop=True,
+                        )
+                m = 2 * a + half
+                nc.scalar.copy(
+                    out=dqs[s][:, m * P : (m + 1) * P, :].rearrange("p (v q) t -> p v q t", v=4),
+                    in_=total[:].rearrange("p v (t q) -> p v q t", t=PACK),
+                )
 
-        def quantise_x(u, x_grouped):
-            both = slice(PAIR * u, PAIR * (u + 1))
+        def load_x(c):
+            x_raw = x_pool.tile([P, PACK, DIM], BF16, name="x_raw")
+            nc.sync.dma_start(out=x_raw[:].rearrange("p t i -> p (t i)"), in_=x_view[c])
+            x_raws[c] = x_raw
+
+        def regroup_x(c, piece):
+            if c not in x_groupeds:
+                x_groupeds[c] = x_pool.tile([P, DIM, PACK], BF16, name="x_grouped", align_bytes=64)
+            cols = slice(piece * (DIM // X_PIECES), (piece + 1) * (DIM // X_PIECES))
+            nc.scalar.copy(out=x_groupeds[c][:, cols, :], in_=x_raws[c][:, :, cols].rearrange("p t i -> p i t"))
+
+        def quantise_x(c):
             nc.vector.quantize_mx(
-                out=x_codes[:, both, :].rearrange("p c i -> p (c i)").bitcast(E4M3_X4),
-                scales=x_scales[:, both, :].rearrange("p c i -> p (c i)"),
-                in_=x_grouped[:].rearrange("p c i t -> p (c i t)"),
+                out=x_codes[:, c, :].bitcast(E4M3_X4),
+                scales=x_scales[:, c, :],
+                in_=x_groupeds[c][:].rearrange("p i t -> p (i t)"),
             )
 
-        def quantise_and_multiply(u, dq, acc):
-            dp_codes = code_pool.tile([P, PAIR, COLS], U32, align_bytes=64)
-            dp_scales = code_pool.tile([P, PAIR, COLS], U8, align_bytes=64)
+        def quantise_dp(s):
+            dp_codes = code_pool.tile([P, COLS], U32, name="dp_codes", align_bytes=64)
+            dp_scales = code_pool.tile([P, COLS], U8, name="dp_scales", align_bytes=64)
             nc.vector.quantize_mx(
-                out=dp_codes[:].rearrange("p c w -> p (c w)").bitcast(E5M2_X4),
-                scales=dp_scales[:].rearrange("p c w -> p (c w)"),
-                in_=dq[:].rearrange("p c h d t -> p (c h d t)"),
+                out=dp_codes[:].bitcast(E5M2_X4),
+                scales=dp_scales[:],
+                in_=dqs[s][:].rearrange("p c t -> p (c t)"),
             )
-            for k in range(PAIR):
-                c = PAIR * u + k
-                for m in range(M_TILES):
-                    cols = slice(m * P, (m + 1) * P)
-                    nc.tensor.matmul_mx(
-                        out=acc[m][:],
-                        lhsT=dp_codes[:, k, cols].bitcast(E5M2_X4),
-                        lhsT_scale=dp_scales[:, k, cols],
-                        rhs=x_codes[:, c, :].bitcast(E4M3_X4),
-                        rhs_scale=x_scales[:, c, :],
-                        start=(c == 0),
-                        stop=(c == PASSES - 1),
-                    )
+            codes[s] = (dp_codes, dp_scales)
 
-        def store_round(r, acc):
+        def multiply(s):
+            r, c = divmod(s, PASSES)
+            if s in first_steps:
+                accs.clear()
+                accs.extend([acc_psum.tile([P, DIM], F32, name="acc%d" % m, tag="acc") for m in range(M_TILES)])
+            dp_codes, dp_scales = codes[s]
             for m in range(M_TILES):
-                rows = slice(r * COLS + m * P, r * COLS + (m + 1) * P)
-                result = res_pool.tile([P, DIM], F32)
-                nc.scalar.copy(out=result[:], in_=acc[m][:])
-                nc.scalar.dma_start(out=out[rows, :], in_=result[:])
+                cols = slice(m * P, (m + 1) * P)
+                nc.tensor.matmul_mx(
+                    out=accs[m][:],
+                    lhsT=dp_codes[:, cols].bitcast(E5M2_X4),
+                    lhsT_scale=dp_scales[:, cols],
+                    rhs=x_codes[:, c, :].bitcast(E4M3_X4),
+                    rhs_scale=x_scales[:, c, :],
+                    start=(s in first_steps),
+                    stop=(s in last_steps),
+                )
+            if s in last_steps:
+                store_round(r)
 
-        def finish(r, u, dq, x_grouped, acc):
-            if r == 0:
-                quantise_x(u, x_grouped)
-            quantise_and_multiply(u, dq, acc)
-            if u == UNITS - 1:
-                store_round(r, acc)
+        def store_round(r):
+            for m in range(M_TILES):
+                result = res_pool.tile([P, DIM], F32, name="result")
+                if m % 2 == 0:
+                    nc.vector.tensor_copy(out=result[:], in_=accs[m][:])
+                else:
+                    nc.scalar.copy(out=result[:], in_=accs[m][:])
+                for v in range(4):
+                    head = r * HEADS + 2 * m + v // 2
+                    nc.sync.dma_start(out=out_view[head, v % 2], in_=result[v * PAIRS : (v + 1) * PAIRS, :])
 
-        units = [(r, u) for r in range(ROUNDS) for u in range(UNITS)]
-        AHEAD = 2
+        def position_of(n):
+            return n + 3 if on_gpsimd(n) else n
+
+        ready_at = [max(position_of(2 * s), position_of(2 * s + 1)) for s in range(STEPS)]
+        in_order = sorted(range(STEPS), key=lambda s: ready_at[s])
+        by_round = [[s for s in in_order if s // PASSES == r] for r in range(ROUNDS)]
+        first_steps = [steps[0] for steps in by_round]
+        last_steps = [steps[-1] for steps in by_round]
+        assert ready_at[last_steps[0]] < ready_at[first_steps[1]]
+
         with tc.manual_schedule():
-            reordered = [reorder_g(*unit) for unit in units[:AHEAD]]
-            x_grouped = regroup_x(0)
-            acc = None
-            added = None
-            for n, (r, u) in enumerate(units):
-                factors = products(u, reordered[n])
-                if added is not None:
-                    finish(*added, acc)
-                if u == 0:
-                    acc = [acc_psum.tile([P, DIM], F32, name="acc%d" % m, tag="acc") for m in range(M_TILES)]
-                if n + AHEAD < len(units):
-                    reordered.append(reorder_g(*units[n + AHEAD]))
-                added = (r, u, add(*factors), x_grouped)
-                x_grouped = regroup_x(u + 1) if r == 0 and u + 1 < UNITS else None
-            finish(*added, acc)
+            load_g(0)
+            load_g(1)
+            load_x(0)
+            load_g(2)
+            load_x(1)
+            load_g(3)
+            load_x(2)
+            for n in (2, 0, 1):
+                turn_and_multiply(n)
+            for piece in range(X_PIECES):
+                regroup_x(0, piece)
+            for i in range(UNITS + 5):
+                n = unit_added_at(i)
+                if n is not None:
+                    add_up(n)
+                if i + 3 < UNITS:
+                    turn_and_multiply(i + 3)
+                if i % 2 == 1 and (i + 7) // 2 < STEPS:
+                    load_g((i + 7) // 2)
+                if i % 2 == 0 and i // 2 + 3 < PASSES:
+                    load_x(i // 2 + 3)
+                if i // 2 + 1 < PASSES:
+                    for piece in (2 * (i % 2), 2 * (i % 2) + 1):
+                        regroup_x(i // 2 + 1, piece)
+                if i % 2 == 1 and i // 2 < PASSES:
+                    quantise_x(i // 2)
+                for s in in_order:
+                    if ready_at[s] == i:
+                        quantise_dp(s)
+                for s in in_order:
+                    if ready_at[s] == i - 2:
+                        multiply(s)

@@ -36,12 +36,15 @@ FLOPS = 2 * T * E * DIM
 BYTES = 2 * (T * DIM + T * E + 2 * S * HD) + 4 * E * DIM
 
 
+GPSIMD_EVERY = 5
+
+
 def on_gpsimd(n):
-    return n % 3 == 2
+    return n % GPSIMD_EVERY == GPSIMD_EVERY - 1
 
 
 def unit_added_at(i):
-    n = i if i % 3 != 2 else i - 3
+    n = i - GPSIMD_EVERY if on_gpsimd(i) else i
     return n if 0 <= n < UNITS else None
 
 
@@ -55,7 +58,8 @@ def tile_attention_pa_k_kernel(tc, query, wq, bq, cos, sin, grad_out, out):
         keep = stack.enter_context(tc.tile_pool(name="keep", bufs=1))
         raw_pool = stack.enter_context(tc.tile_pool(name="g_raw", bufs=4))
         copy_pool = stack.enter_context(tc.tile_pool(name="g_copy", bufs=2))
-        prod_pool = stack.enter_context(tc.tile_pool(name="products", bufs=6))
+        prod_pool = stack.enter_context(tc.tile_pool(name="products", bufs=4))
+        slow_pool = stack.enter_context(tc.tile_pool(name="gpsimd_products", bufs=3))
         x_pool = stack.enter_context(tc.tile_pool(name="x", bufs=3))
         dq_pool = stack.enter_context(tc.tile_pool(name="dq", bufs=4))
         code_pool = stack.enter_context(tc.tile_pool(name="dp_codes", bufs=4))
@@ -121,21 +125,17 @@ def tile_attention_pa_k_kernel(tc, query, wq, bq, cos, sin, grad_out, out):
             g_t = turn_psum.tile([P, QUAD, P], F32, name="g_t", tag="g_t")
             for h in range(QUAD):
                 nc.tensor.transpose(g_t[:, h, :], raws[s][:, a * QUAD + h, :].bitcast(F32), identity[:])
-            with_cos = prod_pool.tile([P, QUAD, 2, P], F32, name="with_cos")
-            with_sin = prod_pool.tile([P, QUAD, 2, P], F32, name="with_sin")
+            pool = slow_pool if on_gpsimd(n) else prod_pool
+            with_cos = pool.tile([P, QUAD, 2, P], F32, name="with_cos")
+            with_sin = pool.tile([P, QUAD, 2, P], F32, name="with_sin")
             terms = ((cos_t, with_cos), (sin_t, with_sin))
             if on_gpsimd(n):
                 g_copy = copy_pool.tile([P, QUAD, P], F32, name="g_copy")
                 nc.scalar.copy(out=g_copy[:], in_=g_t[:])
                 values = parities_apart(g_copy[:], QUAD)
-                for h in range(0, QUAD, 2):
+                for h in range(QUAD):
                     for table, product in terms:
-                        nc.gpsimd.tensor_tensor(
-                            out=product[:, h : h + 2],
-                            in0=values[:, h : h + 2],
-                            in1=table[:, j].unsqueeze(1).to_broadcast([P, 2, 2, P]),
-                            op=MULT,
-                        )
+                        nc.gpsimd.tensor_tensor(out=product[:, h], in0=values[:, h], in1=table[:, j], op=MULT)
             else:
                 values = parities_apart(g_t[:], QUAD)
                 for table, product in terms:
@@ -231,14 +231,19 @@ def tile_attention_pa_k_kernel(tc, query, wq, bq, cos, sin, grad_out, out):
                     nc.sync.dma_start(out=out_view[head, v % 2], in_=result[v * PAIRS : (v + 1) * PAIRS, :])
 
         def position_of(n):
-            return n + 3 if on_gpsimd(n) else n
+            return n + GPSIMD_EVERY if on_gpsimd(n) else n
 
         ready_at = [max(position_of(2 * s), position_of(2 * s + 1)) for s in range(STEPS)]
         in_order = sorted(range(STEPS), key=lambda s: ready_at[s])
         by_round = [[s for s in in_order if s // PASSES == r] for r in range(ROUNDS)]
         first_steps = [steps[0] for steps in by_round]
         last_steps = [steps[-1] for steps in by_round]
-        assert ready_at[last_steps[0]] < ready_at[first_steps[1]]
+        multiply_at = {}
+        latest = 0
+        for steps in by_round:
+            for s in steps:
+                latest = max(latest, ready_at[s] + 2)
+                multiply_at[s] = latest
 
         with tc.manual_schedule():
             load_g(0)
@@ -248,11 +253,11 @@ def tile_attention_pa_k_kernel(tc, query, wq, bq, cos, sin, grad_out, out):
             load_x(1)
             load_g(3)
             load_x(2)
-            for n in (2, 0, 1):
+            for n in (0, 1, 2):
                 turn_and_multiply(n)
             for piece in range(X_PIECES):
                 regroup_x(0, piece)
-            for i in range(UNITS + 5):
+            for i in range(UNITS + GPSIMD_EVERY + 3):
                 n = unit_added_at(i)
                 if n is not None:
                     add_up(n)
@@ -270,6 +275,7 @@ def tile_attention_pa_k_kernel(tc, query, wq, bq, cos, sin, grad_out, out):
                 for s in in_order:
                     if ready_at[s] == i:
                         quantise_dp(s)
-                for s in in_order:
-                    if ready_at[s] == i - 2:
-                        multiply(s)
+                for steps in by_round:
+                    for s in steps:
+                        if multiply_at[s] == i:
+                            multiply(s)

@@ -36,16 +36,15 @@ FLOPS = 2 * T * E * DIM
 BYTES = 2 * (T * DIM + T * E + 2 * S * HD) + 4 * E * DIM
 
 
-GPSIMD_EVERY = 5
+FRAME = 4
 
 
 def on_gpsimd(n):
-    return n % GPSIMD_EVERY == GPSIMD_EVERY - 1
+    return n % FRAME == FRAME - 1 and n < UNITS - FRAME
 
 
-def unit_added_at(i):
-    n = i - GPSIMD_EVERY if on_gpsimd(i) else i
-    return n if 0 <= n < UNITS else None
+def position_of(n):
+    return n + FRAME if on_gpsimd(n) else n
 
 
 def tile_attention_pa_k_kernel(tc, query, wq, bq, cos, sin, grad_out, out):
@@ -106,6 +105,10 @@ def tile_attention_pa_k_kernel(tc, query, wq, bq, cos, sin, grad_out, out):
         cos_t = turn_table(cos_raw, "cos_t")
         sin_t = turn_table(sin_signed, "sin_t")
 
+        gpsimd_waits = keep.tile([P, 1], U32)
+        vector_waits = keep.tile([P, 1], F32)
+        newest_word = []
+
         x_codes = keep.tile([P, PASSES, DIM], U32, align_bytes=64)
         x_scales = keep.tile([P, PASSES, DIM], U8, align_bytes=64)
 
@@ -133,9 +136,15 @@ def tile_attention_pa_k_kernel(tc, query, wq, bq, cos, sin, grad_out, out):
                 g_copy = copy_pool.tile([P, QUAD, P], F32, name="g_copy")
                 nc.scalar.copy(out=g_copy[:], in_=g_t[:])
                 values = parities_apart(g_copy[:], QUAD)
-                for h in range(QUAD):
+                nc.gpsimd.tensor_copy(out=gpsimd_waits[:], in_=newest_word[0])
+                for h in range(0, QUAD, 2):
                     for table, product in terms:
-                        nc.gpsimd.tensor_tensor(out=product[:, h], in0=values[:, h], in1=table[:, j], op=MULT)
+                        nc.gpsimd.tensor_tensor(
+                            out=product[:, h : h + 2],
+                            in0=values[:, h : h + 2],
+                            in1=table[:, j].unsqueeze(1).to_broadcast([P, 2, 2, P]),
+                            op=MULT,
+                        )
             else:
                 values = parities_apart(g_t[:], QUAD)
                 for table, product in terms:
@@ -188,6 +197,8 @@ def tile_attention_pa_k_kernel(tc, query, wq, bq, cos, sin, grad_out, out):
                 scales=x_scales[:, c, :],
                 in_=x_groupeds[c][:].rearrange("p i t -> p (i t)"),
             )
+            newest_word.clear()
+            newest_word.append(x_codes[:, c, 0:1])
 
         def quantise_dp(s):
             dp_codes = code_pool.tile([P, COLS], U32, name="dp_codes", align_bytes=64)
@@ -198,6 +209,8 @@ def tile_attention_pa_k_kernel(tc, query, wq, bq, cos, sin, grad_out, out):
                 in_=dqs[s][:].rearrange("p c t -> p (c t)"),
             )
             codes[s] = (dp_codes, dp_scales)
+            newest_word.clear()
+            newest_word.append(dp_codes[:, 0:1])
 
         def multiply(s):
             r, c = divmod(s, PASSES)
@@ -230,11 +243,10 @@ def tile_attention_pa_k_kernel(tc, query, wq, bq, cos, sin, grad_out, out):
                     head = r * HEADS + 2 * m + v // 2
                     nc.sync.dma_start(out=out_view[head, v % 2], in_=result[v * PAIRS : (v + 1) * PAIRS, :])
 
-        def position_of(n):
-            return n + GPSIMD_EVERY if on_gpsimd(n) else n
-
+        last_frame = UNITS - FRAME
         ready_at = [max(position_of(2 * s), position_of(2 * s + 1)) for s in range(STEPS)]
-        in_order = sorted(range(STEPS), key=lambda s: ready_at[s])
+        quantise_at = [r if r > last_frame else -(-r // FRAME) * FRAME for r in ready_at]
+        in_order = sorted(range(STEPS), key=lambda s: (quantise_at[s], ready_at[s]))
         by_round = [[s for s in in_order if s // PASSES == r] for r in range(ROUNDS)]
         first_steps = [steps[0] for steps in by_round]
         last_steps = [steps[-1] for steps in by_round]
@@ -242,7 +254,7 @@ def tile_attention_pa_k_kernel(tc, query, wq, bq, cos, sin, grad_out, out):
         latest = 0
         for steps in by_round:
             for s in steps:
-                latest = max(latest, ready_at[s] + 2)
+                latest = max(latest + 1, quantise_at[s] + 1)
                 multiply_at[s] = latest
 
         with tc.manual_schedule():
@@ -257,10 +269,19 @@ def tile_attention_pa_k_kernel(tc, query, wq, bq, cos, sin, grad_out, out):
                 turn_and_multiply(n)
             for piece in range(X_PIECES):
                 regroup_x(0, piece)
-            for i in range(UNITS + GPSIMD_EVERY + 3):
-                n = unit_added_at(i)
-                if n is not None:
-                    add_up(n)
+            for i in range(latest + 1):
+                for n in range(UNITS):
+                    if position_of(n) == i:
+                        add_up(n)
+                if i % FRAME == 0 and 0 < i <= last_frame:
+                    nc.vector.tensor_copy(out=vector_waits[:], in_=products[i - 1][1][:, QUAD - 1, 1, P - 1 : P])
+                if i % FRAME == 0:
+                    for c in range(PASSES):
+                        if max(0, i // 2 - 1) <= c <= i // 2:
+                            quantise_x(c)
+                for s in in_order:
+                    if quantise_at[s] == i:
+                        quantise_dp(s)
                 if i + 3 < UNITS:
                     turn_and_multiply(i + 3)
                 if i % 2 == 1 and (i + 7) // 2 < STEPS:
@@ -270,11 +291,6 @@ def tile_attention_pa_k_kernel(tc, query, wq, bq, cos, sin, grad_out, out):
                 if i // 2 + 1 < PASSES:
                     for piece in (2 * (i % 2), 2 * (i % 2) + 1):
                         regroup_x(i // 2 + 1, piece)
-                if i % 2 == 1 and i // 2 < PASSES:
-                    quantise_x(i // 2)
-                for s in in_order:
-                    if ready_at[s] == i:
-                        quantise_dp(s)
                 for steps in by_round:
                     for s in steps:
                         if multiply_at[s] == i:

@@ -36,11 +36,12 @@ FLOPS = 2 * T * E * DIM
 BYTES = 2 * (T * DIM + T * E + 2 * S * HD) + 4 * E * DIM
 
 
-FRAME = 4
+FRAME = 5
+AHEAD = 3
 
 
 def on_gpsimd(n):
-    return n % FRAME == FRAME - 1 and n < UNITS - FRAME
+    return n % FRAME == AHEAD and n < UNITS - FRAME
 
 
 def position_of(n):
@@ -60,7 +61,7 @@ def tile_attention_pa_k_kernel(tc, query, wq, bq, cos, sin, grad_out, out):
         prod_pool = stack.enter_context(tc.tile_pool(name="products", bufs=4))
         slow_pool = stack.enter_context(tc.tile_pool(name="gpsimd_products", bufs=3))
         x_pool = stack.enter_context(tc.tile_pool(name="x", bufs=3))
-        dq_pool = stack.enter_context(tc.tile_pool(name="dq", bufs=4))
+        dq_pool = stack.enter_context(tc.tile_pool(name="dq", bufs=5))
         code_pool = stack.enter_context(tc.tile_pool(name="dp_codes", bufs=4))
         res_pool = stack.enter_context(tc.tile_pool(name="result", bufs=4))
         turn_psum = stack.enter_context(tc.psum_pool(name="turned", bufs=2))
@@ -243,7 +244,7 @@ def tile_attention_pa_k_kernel(tc, query, wq, bq, cos, sin, grad_out, out):
                     head = r * HEADS + 2 * m + v // 2
                     nc.sync.dma_start(out=out_view[head, v % 2], in_=result[v * PAIRS : (v + 1) * PAIRS, :])
 
-        last_frame = UNITS - FRAME
+        last_frame = max(n for n in range(UNITS) if on_gpsimd(n)) - AHEAD + FRAME
         ready_at = [max(position_of(2 * s), position_of(2 * s + 1)) for s in range(STEPS)]
         quantise_at = [r if r > last_frame else -(-r // FRAME) * FRAME for r in ready_at]
         in_order = sorted(range(STEPS), key=lambda s: (quantise_at[s], ready_at[s]))
@@ -274,16 +275,18 @@ def tile_attention_pa_k_kernel(tc, query, wq, bq, cos, sin, grad_out, out):
                     if position_of(n) == i:
                         add_up(n)
                 if i % FRAME == 0 and 0 < i <= last_frame:
-                    nc.vector.tensor_copy(out=vector_waits[:], in_=products[i - 1][1][:, QUAD - 1, 1, P - 1 : P])
+                    nc.vector.tensor_copy(
+                        out=vector_waits[:], in_=products[i - FRAME + AHEAD][1][:, QUAD - 1, 1, P - 1 : P]
+                    )
                 if i % FRAME == 0:
                     for c in range(PASSES):
-                        if max(0, i // 2 - 1) <= c <= i // 2:
+                        if i - FRAME < 2 * c <= i:
                             quantise_x(c)
                 for s in in_order:
                     if quantise_at[s] == i:
                         quantise_dp(s)
-                if i + 3 < UNITS:
-                    turn_and_multiply(i + 3)
+                if i + AHEAD < UNITS:
+                    turn_and_multiply(i + AHEAD)
                 if i % 2 == 1 and (i + 7) // 2 < STEPS:
                     load_g((i + 7) // 2)
                 if i % 2 == 0 and i // 2 + 3 < PASSES:

@@ -62,7 +62,7 @@ def tile_attention_pa_k_kernel(tc, query, wq, bq, cos, sin, grad_out, out):
         slow_pool = stack.enter_context(tc.tile_pool(name="gpsimd_products", bufs=3))
         x_pool = stack.enter_context(tc.tile_pool(name="x", bufs=3))
         dq_pool = stack.enter_context(tc.tile_pool(name="dq", bufs=5))
-        code_pool = stack.enter_context(tc.tile_pool(name="dp_codes", bufs=4))
+        code_pool = stack.enter_context(tc.tile_pool(name="dp_codes", bufs=5))
         res_pool = stack.enter_context(tc.tile_pool(name="result", bufs=4))
         turn_psum = stack.enter_context(tc.psum_pool(name="turned", bufs=2))
         total_psum = stack.enter_context(tc.psum_pool(name="totals", bufs=2))
@@ -114,7 +114,7 @@ def tile_attention_pa_k_kernel(tc, query, wq, bq, cos, sin, grad_out, out):
         x_scales = keep.tile([P, PASSES, DIM], U8, align_bytes=64)
 
         raws, products, dqs, codes, x_raws, x_groupeds = {}, {}, {}, {}, {}, {}
-        accs = []
+        accs = {}
 
         def load_g(s):
             r, c = divmod(s, PASSES)
@@ -213,13 +213,12 @@ def tile_attention_pa_k_kernel(tc, query, wq, bq, cos, sin, grad_out, out):
             newest_word.clear()
             newest_word.append(dp_codes[:, 0:1])
 
-        def multiply(s):
+        def multiply(s, half):
             r, c = divmod(s, PASSES)
-            if s in first_steps:
-                accs.clear()
-                accs.extend([acc_psum.tile([P, DIM], F32, name="acc%d" % m, tag="acc") for m in range(M_TILES)])
             dp_codes, dp_scales = codes[s]
-            for m in range(M_TILES):
+            for m in (2 * half, 2 * half + 1):
+                if s in first_steps:
+                    accs[m] = acc_psum.tile([P, DIM], F32, name="acc%d" % m, tag="acc")
                 cols = slice(m * P, (m + 1) * P)
                 nc.tensor.matmul_mx(
                     out=accs[m][:],
@@ -231,18 +230,18 @@ def tile_attention_pa_k_kernel(tc, query, wq, bq, cos, sin, grad_out, out):
                     stop=(s in last_steps),
                 )
             if s in last_steps:
-                store_round(r)
+                for m in (2 * half, 2 * half + 1):
+                    store(r, m)
 
-        def store_round(r):
-            for m in range(M_TILES):
-                result = res_pool.tile([P, DIM], F32, name="result")
-                if m % 2 == 0:
-                    nc.vector.tensor_copy(out=result[:], in_=accs[m][:])
-                else:
-                    nc.scalar.copy(out=result[:], in_=accs[m][:])
-                for v in range(4):
-                    head = r * HEADS + 2 * m + v // 2
-                    nc.sync.dma_start(out=out_view[head, v % 2], in_=result[v * PAIRS : (v + 1) * PAIRS, :])
+        def store(r, m):
+            result = res_pool.tile([P, DIM], F32, name="result")
+            if m % 2 == 0 and r == ROUNDS - 1:
+                nc.vector.tensor_copy(out=result[:], in_=accs[m][:])
+            else:
+                nc.scalar.copy(out=result[:], in_=accs[m][:])
+            for v in range(4):
+                head = r * HEADS + 2 * m + v // 2
+                nc.sync.dma_start(out=out_view[head, v % 2], in_=result[v * PAIRS : (v + 1) * PAIRS, :])
 
         last_frame = max(n for n in range(UNITS) if on_gpsimd(n)) - AHEAD + FRAME
         ready_at = [max(position_of(2 * s), position_of(2 * s + 1)) for s in range(STEPS)]
@@ -256,7 +255,10 @@ def tile_attention_pa_k_kernel(tc, query, wq, bq, cos, sin, grad_out, out):
         for steps in by_round:
             for s in steps:
                 latest = max(latest + 1, quantise_at[s] + 1)
-                multiply_at[s] = latest
+                multiply_at[(s, 0)] = latest
+                if latest < UNITS - 2 * FRAME:
+                    latest += 1
+                multiply_at[(s, 1)] = latest
 
         with tc.manual_schedule():
             load_g(0)
@@ -296,5 +298,6 @@ def tile_attention_pa_k_kernel(tc, query, wq, bq, cos, sin, grad_out, out):
                         regroup_x(i // 2 + 1, piece)
                 for steps in by_round:
                     for s in steps:
-                        if multiply_at[s] == i:
-                            multiply(s)
+                        for half in range(2):
+                            if multiply_at[(s, half)] == i:
+                                multiply(s, half)

@@ -123,10 +123,13 @@ def tile_attention_pa_k_kernel(tc, query, wq, bq, cos, sin, grad_out, out):
             nc.sync.dma_start(out=g_raw[:], in_=g_view[b, j][:, r * HEADS : (r + 1) * HEADS, :])
             raws[s] = g_raw
 
-        def turn_and_multiply(n):
+        def turn_and_multiply(n, keep_clock_up):
             s, a = divmod(n, 2)
             j = s % GROUPS
             g_t = turn_psum.tile([P, QUAD, P], F32, name="g_t", tag="g_t")
+            if keep_clock_up:
+                for h in range(2):
+                    nc.tensor.matmul(out=g_t[:, h, :], lhsT=identity[:], rhs=swap[:], start=True, stop=True)
             for h in range(QUAD):
                 nc.tensor.transpose(g_t[:, h, :], raws[s][:, a * QUAD + h, :].bitcast(F32), identity[:])
             pool = slow_pool if on_gpsimd(n) else prod_pool
@@ -251,14 +254,17 @@ def tile_attention_pa_k_kernel(tc, query, wq, bq, cos, sin, grad_out, out):
         first_steps = [steps[0] for steps in by_round]
         last_steps = [steps[-1] for steps in by_round]
         multiply_at = {}
+        with_matmul_mx = set()
         latest = 0
         for steps in by_round:
             for s in steps:
                 latest = max(latest + 1, quantise_at[s] + 1)
                 multiply_at[(s, 0)] = latest
-                if latest < UNITS - 2 * FRAME:
+                with_matmul_mx.add(latest)
+                if latest < last_frame:
                     latest += 1
                 multiply_at[(s, 1)] = latest
+                with_matmul_mx.add(latest)
 
         with tc.manual_schedule():
             load_g(0)
@@ -269,7 +275,7 @@ def tile_attention_pa_k_kernel(tc, query, wq, bq, cos, sin, grad_out, out):
             load_g(3)
             load_x(2)
             for n in (0, 1, 2):
-                turn_and_multiply(n)
+                turn_and_multiply(n, False)
             for piece in range(X_PIECES):
                 regroup_x(0, piece)
             for i in range(latest + 1):
@@ -288,7 +294,7 @@ def tile_attention_pa_k_kernel(tc, query, wq, bq, cos, sin, grad_out, out):
                     if quantise_at[s] == i:
                         quantise_dp(s)
                 if i + AHEAD < UNITS:
-                    turn_and_multiply(i + AHEAD)
+                    turn_and_multiply(i + AHEAD, i not in with_matmul_mx)
                 if i % 2 == 1 and (i + 7) // 2 < STEPS:
                     load_g((i + 7) // 2)
                 if i % 2 == 0 and i // 2 + 3 < PASSES:

from contextlib import ExitStack

import concourse.mybir as mybir
from concourse.masks import make_identity

BF16 = mybir.dt.bfloat16
F32 = mybir.dt.float32
U32 = mybir.dt.uint32
U8 = mybir.dt.uint8
E4M3_X4 = mybir.dt.float8_e4m3fn_x4
E5M2_X4 = mybir.dt.float8_e5m2_x4
MULT = mybir.AluOpType.mult

B, S, DIM, H, HD = 4, 2048, 512, 16, 64
E = H * HD
T = B * S
HALF = HD // 2

P = 128
PACK = 4
K_PASS = P * PACK
GROUPS = S // K_PASS
PASSES = B * GROUPS
PAIRS = HD // 2

ROUNDS = 2
HEADS = H // ROUNDS
COLS = HEADS * HD
M_TILES = COLS // P
QUAD = 4
UNITS = ROUNDS * PASSES * (HEADS // QUAD)
STEPS = ROUNDS * PASSES
X_PIECES = 4

FLOPS = 2 * T * E * DIM
BYTES = 2 * (T * DIM + T * E + 2 * S * HD) + 4 * E * DIM


FRAME = 5
AHEAD = 3


def on_gpsimd(n):
    return n % FRAME == AHEAD and n < UNITS - FRAME


def position_of(n):
    return n + FRAME if on_gpsimd(n) else n


def tile_attention_pa_k_kernel(tc, query, wq, bq, cos, sin, grad_out, out):
    nc = tc.nc
    x_view = query.rearrange("b (j p t) i -> (b j) p (t i)", p=P, t=PACK)
    g_view = grad_out.rearrange("b h (j p t) d -> b j p h (t d)", p=P, t=PACK)
    out_view = out.rearrange("(a q e) i -> a e q i", q=PAIRS, e=2)

    with ExitStack() as stack:
        keep = stack.enter_context(tc.tile_pool(name="keep", bufs=1))
        raw_pool = stack.enter_context(tc.tile_pool(name="g_raw", bufs=4))
        copy_pool = stack.enter_context(tc.tile_pool(name="g_copy", bufs=2))
        prod_pool = stack.enter_context(tc.tile_pool(name="products", bufs=4))
        slow_pool = stack.enter_context(tc.tile_pool(name="gpsimd_products", bufs=3))
        x_pool = stack.enter_context(tc.tile_pool(name="x", bufs=3))
        dq_pool = stack.enter_context(tc.tile_pool(name="dq", bufs=5))
        code_pool = stack.enter_context(tc.tile_pool(name="dp_codes", bufs=5))
        res_pool = stack.enter_context(tc.tile_pool(name="result", bufs=4))
        turn_psum = stack.enter_context(tc.psum_pool(name="turned", bufs=2))
        total_psum = stack.enter_context(tc.psum_pool(name="totals", bufs=2))
        acc_psum = stack.enter_context(tc.psum_pool(name="acc", bufs=M_TILES))

        def load_table(table):
            raw = keep.tile([P, GROUPS, PACK, HD], BF16, name="raw_table", tag="raw_table", bufs=2)
            nc.sync.dma_start(
                out=raw[:].rearrange("p j t d -> p j (t d)"),
                in_=table[0, 0].rearrange("(j p t) d -> p j (t d)", p=P, t=PACK),
            )
            return raw

        cos_raw = load_table(cos)
        sin_raw = load_table(sin)

        identity = keep.tile([P, P], F32)
        make_identity(nc, identity[:])
        swap = keep.tile([P, P], F32)
        identity_blocks = identity[:].rearrange("k (t u w) -> k t u w", t=PACK, u=2)
        swap_blocks = swap[:].rearrange("k (t u w) -> k t u w", t=PACK, u=2)
        nc.vector.tensor_copy(out=swap_blocks[:, :, 0, :], in_=identity_blocks[:, :, 1, :])
        nc.vector.tensor_copy(out=swap_blocks[:, :, 1, :], in_=identity_blocks[:, :, 0, :])

        sin_signed = keep.tile([P, GROUPS, PACK, HD], BF16)
        nc.vector.tensor_scalar_mul(sin_signed[:, :, :, :HALF], sin_raw[:, :, :, :HALF], -1.0)
        nc.vector.tensor_copy(out=sin_signed[:, :, :, HALF:], in_=sin_raw[:, :, :, HALF:])

        def parities_apart(words, count):
            flat = words.rearrange("k c p -> k (c p)").bitcast(BF16)
            return flat.rearrange("k (c p e) -> k c e p", c=count, e=2)

        def turn_table(raw, name):
            bank = turn_psum.tile([P, GROUPS, P], F32, name="g_t", tag="g_t")
            for j in range(GROUPS):
                nc.tensor.transpose(bank[:, j, :], raw[:, j].rearrange("p t d -> p (t d)").bitcast(F32), identity[:])
            table = keep.tile([P, GROUPS, 2, P], BF16, name=name)
            nc.vector.tensor_copy(out=table[:], in_=parities_apart(bank[:], GROUPS))
            return table

        cos_t = turn_table(cos_raw, "cos_t")
        sin_t = turn_table(sin_signed, "sin_t")

        gpsimd_waits = keep.tile([P, 1], U32)
        vector_waits = keep.tile([P, 1], F32)
        newest_word = []

        x_codes = keep.tile([P, PASSES, DIM], U32, align_bytes=64)
        x_scales = keep.tile([P, PASSES, DIM], U8, align_bytes=64)

        raws, products, dqs, codes, x_raws, x_groupeds = {}, {}, {}, {}, {}, {}
        accs = {}

        def load_g(s):
            r, c = divmod(s, PASSES)
            b, j = divmod(c, GROUPS)
            g_raw = raw_pool.tile([P, HEADS, PACK * HD], BF16, name="g_raw")
            nc.sync.dma_start(out=g_raw[:], in_=g_view[b, j][:, r * HEADS : (r + 1) * HEADS, :])
            raws[s] = g_raw

        def turn_and_multiply(n, keep_clock_up):
            s, a = divmod(n, 2)
            j = s % GROUPS
            g_t = turn_psum.tile([P, QUAD, P], F32, name="g_t", tag="g_t")
            if keep_clock_up:
                for h in range(2):
                    nc.tensor.matmul(out=g_t[:, h, :], lhsT=identity[:], rhs=swap[:], start=True, stop=True)
            for h in range(QUAD):
                nc.tensor.transpose(g_t[:, h, :], raws[s][:, a * QUAD + h, :].bitcast(F32), identity[:])
            pool = slow_pool if on_gpsimd(n) else prod_pool
            with_cos = pool.tile([P, QUAD, 2, P], F32, name="with_cos")
            with_sin = pool.tile([P, QUAD, 2, P], F32, name="with_sin")
            terms = ((cos_t, with_cos), (sin_t, with_sin))
            if on_gpsimd(n):
                g_copy = copy_pool.tile([P, QUAD, P], F32, name="g_copy")
                nc.scalar.copy(out=g_copy[:], in_=g_t[:])
                values = parities_apart(g_copy[:], QUAD)
                nc.gpsimd.tensor_copy(out=gpsimd_waits[:], in_=newest_word[0])
                for h in range(0, QUAD, 2):
                    for table, product in terms:
                        nc.gpsimd.tensor_tensor(
                            out=product[:, h : h + 2],
                            in0=values[:, h : h + 2],
                            in1=table[:, j].unsqueeze(1).to_broadcast([P, 2, 2, P]),
                            op=MULT,
                        )
            else:
                values = parities_apart(g_t[:], QUAD)
                for table, product in terms:
                    nc.vector.tensor_tensor(
                        out=product[:],
                        in0=values,
                        in1=table[:, j].unsqueeze(1).to_broadcast([P, QUAD, 2, P]),
                        op=MULT,
                    )
            products[n] = (with_cos, with_sin)

        def add_up(n):
            s, a = divmod(n, 2)
            if s not in dqs:
                dqs[s] = dq_pool.tile([P, COLS, PACK], BF16, name="dq", align_bytes=64)
            with_cos, with_sin = products[n]
            for half in range(2):
                total = total_psum.tile([P, 4, P], F32, name="total")
                for h2 in range(2):
                    for e in range(2):
                        h = 2 * half + h2
                        nc.tensor.matmul(
                            out=total[:, 2 * h2 + e, :], lhsT=with_cos[:, h, e, :], rhs=identity[:],
                            is_transpose=True, start=True, stop=False,
                        )
                        nc.tensor.matmul(
                            out=total[:, 2 * h2 + e, :], lhsT=with_sin[:, h, e, :], rhs=swap[:],
                            is_transpose=True, start=False, stop=True,
                        )
                m = 2 * a + half
                nc.scalar.copy(
                    out=dqs[s][:, m * P : (m + 1) * P, :].rearrange("p (v q) t -> p v q t", v=4),
                    in_=total[:].rearrange("p v (t q) -> p v q t", t=PACK),
                )

        def load_x(c):
            x_raw = x_pool.tile([P, PACK, DIM], BF16, name="x_raw")
            nc.sync.dma_start(out=x_raw[:].rearrange("p t i -> p (t i)"), in_=x_view[c])
            x_raws[c] = x_raw

        def regroup_x(c, piece):
            if c not in x_groupeds:
                x_groupeds[c] = x_pool.tile([P, DIM, PACK], BF16, name="x_grouped", align_bytes=64)
            cols = slice(piece * (DIM // X_PIECES), (piece + 1) * (DIM // X_PIECES))
            nc.scalar.copy(out=x_groupeds[c][:, cols, :], in_=x_raws[c][:, :, cols].rearrange("p t i -> p i t"))

        def quantise_x(c):
            nc.vector.quantize_mx(
                out=x_codes[:, c, :].bitcast(E4M3_X4),
                scales=x_scales[:, c, :],
                in_=x_groupeds[c][:].rearrange("p i t -> p (i t)"),
            )
            newest_word.clear()
            newest_word.append(x_codes[:, c, 0:1])

        def quantise_dp(s):
            dp_codes = code_pool.tile([P, COLS], U32, name="dp_codes", align_bytes=64)
            dp_scales = code_pool.tile([P, COLS], U8, name="dp_scales", align_bytes=64)
            nc.vector.quantize_mx(
                out=dp_codes[:].bitcast(E5M2_X4),
                scales=dp_scales[:],
                in_=dqs[s][:].rearrange("p c t -> p (c t)"),
            )
            codes[s] = (dp_codes, dp_scales)
            newest_word.clear()
            newest_word.append(dp_codes[:, 0:1])

        def multiply(s, half):
            r, c = divmod(s, PASSES)
            dp_codes, dp_scales = codes[s]
            for m in (2 * half, 2 * half + 1):
                if s in first_steps:
                    accs[m] = acc_psum.tile([P, DIM], F32, name="acc%d" % m, tag="acc")
                cols = slice(m * P, (m + 1) * P)
                nc.tensor.matmul_mx(
                    out=accs[m][:],
                    lhsT=dp_codes[:, cols].bitcast(E5M2_X4),
                    lhsT_scale=dp_scales[:, cols],
                    rhs=x_codes[:, c, :].bitcast(E4M3_X4),
                    rhs_scale=x_scales[:, c, :],
                    start=(s in first_steps),
                    stop=(s in last_steps),
                )
            if s in last_steps:
                for m in (2 * half, 2 * half + 1):
                    store(r, m)

        def store(r, m):
            result = res_pool.tile([P, DIM], F32, name="result")
            if m % 2 == 0 and r == ROUNDS - 1:
                nc.vector.tensor_copy(out=result[:], in_=accs[m][:])
            else:
                nc.scalar.copy(out=result[:], in_=accs[m][:])
            for v in range(4):
                head = r * HEADS + 2 * m + v // 2
                nc.sync.dma_start(out=out_view[head, v % 2], in_=result[v * PAIRS : (v + 1) * PAIRS, :])

        last_frame = max(n for n in range(UNITS) if on_gpsimd(n)) - AHEAD + FRAME
        ready_at = [max(position_of(2 * s), position_of(2 * s + 1)) for s in range(STEPS)]
        quantise_at = [r if r > last_frame else -(-r // FRAME) * FRAME for r in ready_at]
        in_order = sorted(range(STEPS), key=lambda s: (quantise_at[s], ready_at[s]))
        by_round = [[s for s in in_order if s // PASSES == r] for r in range(ROUNDS)]
        first_steps = [steps[0] for steps in by_round]
        last_steps = [steps[-1] for steps in by_round]
        multiply_at = {}
        with_matmul_mx = set()
        latest = 0
        for steps in by_round:
            for s in steps:
                latest = max(latest + 1, quantise_at[s] + 1)
                multiply_at[(s, 0)] = latest
                with_matmul_mx.add(latest)
                if latest < last_frame:
                    latest += 1
                multiply_at[(s, 1)] = latest
                with_matmul_mx.add(latest)

        with tc.manual_schedule():
            load_g(0)
            load_g(1)
            load_x(0)
            load_g(2)
            load_x(1)
            load_g(3)
            load_x(2)
            for n in (0, 1, 2):
                turn_and_multiply(n, False)
            for piece in range(X_PIECES):
                regroup_x(0, piece)
            for i in range(latest + 1):
                for n in range(UNITS):
                    if position_of(n) == i:
                        add_up(n)
                if i % FRAME == 0 and 0 < i <= last_frame:
                    nc.vector.tensor_copy(
                        out=vector_waits[:], in_=products[i - FRAME + AHEAD][1][:, QUAD - 1, 1, P - 1 : P]
                    )
                if i % FRAME == 0:
                    for c in range(PASSES):
                        if i - FRAME < 2 * c <= i:
                            quantise_x(c)
                for s in in_order:
                    if quantise_at[s] == i:
                        quantise_dp(s)
                if i + AHEAD < UNITS:
                    turn_and_multiply(i + AHEAD, i not in with_matmul_mx)
                if i % 2 == 1 and (i + 7) // 2 < STEPS:
                    load_g((i + 7) // 2)
                if i % 2 == 0 and i // 2 + 3 < PASSES:
                    load_x(i // 2 + 3)
                if i // 2 + 1 < PASSES:
                    for piece in (2 * (i % 2), 2 * (i % 2) + 1):
                        regroup_x(i // 2 + 1, piece)
                for steps in by_round:
                    for s in steps:
                        for half in range(2):
                            if multiply_at[(s, half)] == i:
                                multiply(s, half)
